import numpy as np
import ml_dtypes


def mxq(x, axis, fmt="e4m3"):
    dtype, down = {"e4m3": (ml_dtypes.float8_e4m3fn, 7), "e5m2": (ml_dtypes.float8_e5m2, 14)}[fmt]
    v = np.moveaxis(np.asarray(x, np.float32).astype(ml_dtypes.bfloat16).astype(np.float64), axis, -1)
    blocks = v.reshape(v.shape[:-1] + (-1, 32))
    amax = np.abs(blocks).max(-1, keepdims=True)
    byte = np.maximum(np.where(amax > 0, np.frexp(amax)[1] - 1 + 127, 0) - down, 1)
    scale = np.exp2(byte - 127.0)
    codes = (blocks / scale).astype(np.float32).astype(dtype).astype(np.float64)
    return np.moveaxis((codes * scale).reshape(v.shape), -1, axis)


WIDE = False


def mx_kscale(k):
    if not WIDE:
        return np.ones(k)
    levels = np.array([10, -10, 5, -5, 0])
    a = np.random.permutation(np.resize(levels, k // 512 * 4)).reshape(k // 512, 4)
    idx = np.arange(k)
    return np.exp2(a[idx // 512, idx % 128 // 32])


BF16 = ml_dtypes.bfloat16


def bf(x):
    return np.asarray(x, np.float32).astype(BF16)


def f64(x):
    return np.asarray(x).astype(np.float64)


B, D, C, T, DEPTH = 4096, 512, 1024, 256, 2
NI = 2 ** DEPTH - 1
NL = 2 ** DEPTH


def sigmoid(v):
    return 1.0 / (1.0 + np.exp(-v))


def softmax(v, axis):
    e = np.exp(v - v.max(axis=axis, keepdims=True))
    return e / e.sum(axis=axis, keepdims=True)


def setup_inputs():
    s = mx_kscale(D)
    return {
        "x": bf(np.random.standard_normal((B, D)) * s),
        "split_weights": bf(np.random.standard_normal((T, NI, D)) * 1.5 / np.sqrt(D) / s),
        "split_biases": bf(np.random.standard_normal((T, NI)) * 0.3),
        "leaf_logits": bf(np.random.standard_normal((T, NL, C)) * 3.0),
        "tree_weights": bf(1.0 / T + 0.5 * np.random.standard_normal(T)),
        "log_temperature": bf(0.3 + 0.1 * np.random.standard_normal(1)),
    }


def reference(x, split_weights, split_biases, leaf_logits, tree_weights, log_temperature):
    x = f64(x)
    split_weights = f64(split_weights)
    leaf_logits = f64(leaf_logits)
    b = x.shape[0]
    t, ni, dd = split_weights.shape
    nl, c = leaf_logits.shape[1], leaf_logits.shape[2]
    depth = int(np.log2(nl))
    temp = np.clip(np.exp(f64(log_temperature)), 0.1, 5.0)
    prod = mxq(x, 1, "e4m3") @ mxq(split_weights, 2, "e4m3").reshape(t * ni, dd).T
    logits = prod.reshape(b, t, ni) + f64(split_biases)[None, :, :]
    s = sigmoid(logits / temp)
    mu = np.ones((b, t, 1))
    for d in range(depth):
        lvl = s[:, :, 2 ** d - 1: 2 ** (d + 1) - 1]
        mu = np.stack([mu * (1.0 - lvl), mu * lvl], axis=-1).reshape(b, t, 2 ** (d + 1))
    leaf_class_probs = softmax(leaf_logits / temp, -1)
    w = softmax(f64(tree_weights), 0)
    a = (mu * w[None, :, None]).reshape(b, t * nl)
    return mxq(a, 1, "e4m3") @ mxq(leaf_class_probs.reshape(t * nl, c), 0, "e4m3")

@@ -1,0 +1,349 @@
+from contextlib import ExitStack
+
+import concourse.masks as masks
+import concourse.mybir as mybir
+
+F32 = mybir.dt.float32
+BF16 = mybir.dt.bfloat16
+U32 = mybir.dt.uint32
+U8 = mybir.dt.uint8
+FP8X4 = mybir.dt.float8_e4m3fn_x4
+AF = mybir.ActivationFunctionType
+ALU = mybir.AluOpType
+AX = mybir.AxisListType
+
+P = 128
+B, D, C, T = 4096, 512, 1024, 256
+NB = 512
+NCH = B // NB
+FLOPS = 2 * B * D * (3 * T) + 2 * B * (4 * T) * C
+
+MANUAL = True
+VEC_SHARE = {6: (5, 7), 7: (1, 3, 5, 7)}
+
+
+def tile_directsofttreeensemble_t_kernel(
+    tc, x, split_weights, split_biases, leaf_logits, tree_weights, log_temperature, out
+):
+    nc = tc.nc
+    with ExitStack() as ctx:
+        if MANUAL:
+            ctx.enter_context(tc.manual_schedule())
+        const = ctx.enter_context(tc.tile_pool(name="const", bufs=1))
+        work = ctx.enter_context(tc.tile_pool(name="work", bufs=2))
+        psum = ctx.enter_context(tc.psum_pool(name="psum", bufs=8))
+
+        ident = const.tile([P, P], F32, name="ident")
+        masks.make_identity(nc, ident[:])
+
+        lt_b = const.tile([P, 1], BF16, name="lt_b")
+        tw_b = const.tile([P, T], BF16, name="tw_b")
+        tw_p = const.tile([P, 2], BF16, name="tw_p")
+        sb = const.tile([P, 6], BF16, name="sb")
+        etemp = const.tile([P, 1], F32, name="etemp")
+        temp = const.tile([P, 1], F32, name="temp")
+        rtemp = const.tile([P, 1], F32, name="rtemp")
+        bt = const.tile([P, 6], F32, name="bt")
+        twm = const.tile([P, 1], F32, name="twm")
+        ntwm = const.tile([P, 1], F32, name="ntwm")
+        twx = const.tile([P, T], F32, name="twx")
+        twsum = const.tile([P, 1], F32, name="twsum")
+        rtw = const.tile([P, 1], F32, name="rtw")
+        twe = const.tile([P, 2], F32, name="twe")
+        wpos = const.tile([P, 2], F32, name="wpos")
+        wneg = const.tile([P, 2], F32, name="wneg")
+        nmax = const.tile([P, 8], F32, name="nmax")
+        sums = const.tile([P, 8], F32, name="sums")
+        rinv = const.tile([P, 8], F32, name="rinv")
+        wc = const.tile([P, 768], U32, name="wc", align_bytes=64)
+        ws = const.tile([P, 768], U8, name="ws", align_bytes=64)
+        pc = const.tile([P, 2048], U32, name="pc", align_bytes=64)
+        ps = const.tile([P, 2048], U8, name="ps", align_bytes=64)
+
+        nc.scalar.dma_start(out=lt_b[:], in_=log_temperature.partition_broadcast(P))
+        nc.scalar.dma_start(out=tw_b[:], in_=tree_weights.partition_broadcast(P))
+        nc.scalar.dma_start(out=tw_p[:], in_=tree_weights.rearrange("(p t) -> p t", t=2))
+        nc.scalar.dma_start(out=sb[:], in_=split_biases.rearrange("(p t) i -> p (t i)", t=2))
+
+        leaf_v = leaf_logits.rearrange("(p t) (h e) c -> p (t h) e c", t=2, e=2)
+        leaf_t = []
+        for k in range(4):
+            lp = work.tile([P, 2048], BF16, tag="raw", bufs=8, name="lp")
+            nc.sync.dma_start(
+                out=lp[:].rearrange("p (r c) -> p r c", r=2),
+                in_=leaf_v[:, 2 * (k % 2) : 2 * (k % 2) + 2, k // 2, :],
+            )
+            leaf_t.append(lp)
+        w_v = split_weights.rearrange("(p t) i d -> p (t i d)", t=2)
+        w_t = []
+        for k in range(2):
+            wr = work.tile([P, 2048], BF16, tag="raw", bufs=8, name="wr")
+            nc.sync.dma_start(out=wr[:, 0:1536], in_=w_v[:, 1536 * k : 1536 * (k + 1)])
+            w_t.append(wr)
+        x_v = x.rearrange("(c p t) d -> c p (t d)", p=P, t=4)
+        out_v = out.rearrange("(c p t) n -> c p (t n)", p=P, t=4)
+        x_t = []
+
+        def x_load():
+            xr = work.tile([P, 2048], BF16, tag="raw", bufs=8, name="xr")
+            nc.sync.dma_start(out=xr[:], in_=x_v[len(x_t)])
+            x_t.append(xr)
+
+        x_load()
+        x_load()
+
+        def transpose_bank(sources):
+            bank = psum.tile([P, 512], F32, tag="bank", name="tbank")
+            for tt in range(2):
+                src, blk = sources[tt]
+                src32 = src[:].bitcast(F32)
+                for u in range(2):
+                    s = 2 * tt + u
+                    nc.tensor.transpose(
+                        out=bank[:, 128 * s : 128 * (s + 1)],
+                        in_=src32[:, 256 * blk + 128 * u : 256 * blk + 128 * (u + 1)],
+                        identity=ident[:],
+                    )
+            return bank
+
+        def regroup(dst32, bank):
+            nc.scalar.copy(
+                out=dst32.rearrange("q (t b u) -> q t b u", t=2, u=2),
+                in_=bank[:].rearrange("q (t u b) -> q t b u", t=2, u=2),
+            )
+
+        def leaf_max(k):
+            e, jj = k // 2, k % 2
+            lp3 = leaf_t[k][:].rearrange("p (r c) -> p r c", r=2)
+            m1 = work.tile([P, 2, 512], BF16, tag="m1", name="m1")
+            nc.vector.tensor_tensor(out=m1[:], in0=lp3[:, :, 0:512], in1=lp3[:, :, 512:1024], op=ALU.max)
+            m2 = work.tile([P, 2, 256], BF16, tag="m2", name="m2")
+            nc.vector.tensor_tensor(out=m2[:], in0=m1[:, :, 0:256], in1=m1[:, :, 256:512], op=ALU.max)
+            mx = work.tile([P, 2], F32, tag="mx", name="mx")
+            nc.vector.tensor_reduce(out=mx[:], in_=m2[:], axis=AX.X, op=ALU.max)
+            col = 4 * e + 2 * jj
+            nc.vector.tensor_scalar(
+                out=nmax[:, col : col + 2], in0=mx[:], scalar1=rtemp[:, 0:1], scalar2=-1.0,
+                op0=ALU.mult, op1=ALU.mult,
+            )
+
+        ee_t = {}
+
+        def leaf_exp(k):
+            e, jj = k // 2, k % 2
+            if jj == 0:
+                ee_t[e] = work.tile([P, 4096], F32, tag="ost", bufs=3, name="ee")
+            for r in range(2):
+                j = 2 * jj + r
+                col = 4 * e + j
+                nc.scalar.activation(
+                    out=ee_t[e][:, 1024 * j : 1024 * (j + 1)],
+                    in_=leaf_t[k][:, 1024 * r : 1024 * (r + 1)],
+                    func=AF.Exp,
+                    bias=nmax[:, col : col + 1],
+                    scale=rtemp[:, 0:1],
+                    accum_out=sums[:, col : col + 1],
+                )
+
+        pg_t = {}
+
+        def leaf_rinv(e):
+            nc.vector.reciprocal(out=rinv[:, 4 * e : 4 * e + 4], in_=sums[:, 4 * e : 4 * e + 4])
+            pg_t[e] = work.tile([P, 4096], BF16, tag="ag", bufs=3, name="pg", align_bytes=64)
+
+        def leaf_norm(e, half):
+            nc.vector.tensor_tensor(
+                out=pg_t[e][:, 2048 * half : 2048 * (half + 1)].rearrange("p (c j) -> p c j", j=4),
+                in0=ee_t[e][:].rearrange("p (j c) -> p c j", j=4)[:, 512 * half : 512 * (half + 1), :],
+                in1=rinv[:, 4 * e : 4 * e + 4].unsqueeze(1).to_broadcast([P, 512, 4]),
+                op=ALU.mult,
+            )
+
+        def leaf_quant(e):
+            nc.vector.quantize_mx(
+                out=pc[:, 1024 * e : 1024 * (e + 1)].bitcast(FP8X4),
+                scales=ps[:, 1024 * e : 1024 * (e + 1)],
+                in_=pg_t[e][:],
+            )
+
+        xbank, xg_t, xc_t, xs_t = {}, {}, {}, {}
+
+        def x_transpose(c):
+            xbank[c] = [transpose_bank([(x_t[c], 2 * g), (x_t[c], 2 * g + 1)]) for g in range(2)]
+
+        def x_regroup(c):
+            xg_t[c] = work.tile([P, 2048], BF16, tag="xg", bufs=2, name="xg", align_bytes=64)
+            xg32 = xg_t[c][:].bitcast(F32)
+            for g in range(2):
+                regroup(xg32[:, 512 * g : 512 * (g + 1)], xbank[c][g])
+
+        def x_quant(c):
+            xc_t[c] = work.tile([P, 512], U32, tag="xc", bufs=3, name="xc", align_bytes=64)
+            xs_t[c] = work.tile([P, 512], U8, tag="xs", bufs=3, name="xs", align_bytes=64)
+            nc.vector.quantize_mx(out=xc_t[c][:].bitcast(FP8X4), scales=xs_t[c][:], in_=xg_t[c][:])
+
+        root_t, child_t, nn_t, ag_t, ac_t, as_t = {}, {}, {}, {}, {}, {}
+
+        def logits_sigmoid(c):
+            root_t[c] = work.tile([P, 1024], F32, tag="root", bufs=3, name="root")
+            child_t[c] = work.tile([P, 2048], F32, tag="child", bufs=3, name="child")
+            for m in (0, 3, 1, 2, 4, 5):
+                th, i = m // 3, m % 3
+                bank = psum.tile([P, 512], F32, tag="bank", name="zbank")
+                nc.tensor.matmul_mx(
+                    out=bank[:],
+                    lhsT=wc[:, 128 * m : 128 * (m + 1)].bitcast(FP8X4),
+                    lhsT_scale=ws[:, 128 * m : 128 * (m + 1)],
+                    rhs=xc_t[c][:].bitcast(FP8X4),
+                    rhs_scale=xs_t[c][:],
+                    start=True,
+                    stop=True,
+                )
+                if i == 0:
+                    dst = root_t[c][:, 512 * th : 512 * (th + 1)]
+                else:
+                    j = 2 * th + i - 1
+                    dst = child_t[c][:, 512 * j : 512 * (j + 1)]
+                nc.scalar.activation(
+                    out=dst, in_=bank[:], func=AF.Sigmoid, bias=bt[:, m : m + 1], scale=rtemp[:, 0:1]
+                )
+
+        def root_planes(c):
+            nn_t[c] = work.tile([P, 2048], F32, tag="nn", bufs=2, name="nn")
+            for th in range(2):
+                s0 = root_t[c][:, 512 * th : 512 * (th + 1)]
+                nc.vector.tensor_scalar(
+                    out=nn_t[c][:, 512 * (2 * th) : 512 * (2 * th + 1)], in0=s0,
+                    scalar1=-1.0, scalar2=wpos[:, th : th + 1], op0=ALU.add, op1=ALU.mult,
+                )
+                nc.vector.tensor_scalar(
+                    out=nn_t[c][:, 512 * (2 * th + 1) : 512 * (2 * th + 2)], in0=s0,
+                    scalar1=wneg[:, th : th + 1], scalar2=None, op0=ALU.mult,
+                )
+
+        def path_products(c):
+            ag_t[c] = work.tile([P, 4096], BF16, tag="ag", bufs=3, name="ag", align_bytes=64)
+            for e in range(2):
+                nc.vector.scalar_tensor_tensor(
+                    out=ag_t[c][:, 2048 * e : 2048 * (e + 1)].rearrange("p (b j) -> p b j", j=4),
+                    in0=child_t[c][:].rearrange("p (j b) -> p b j", j=4),
+                    scalar=-1.0,
+                    in1=nn_t[c][:].rearrange("p (j b) -> p b j", j=4),
+                    op0=(ALU.mult if e == 1 else ALU.add),
+                    op1=ALU.mult,
+                )
+
+        def a_quant(c):
+            ac_t[c] = work.tile([P, 1024], U32, tag="ac", bufs=4, name="ac", align_bytes=64)
+            as_t[c] = work.tile([P, 1024], U8, tag="as", bufs=4, name="asc", align_bytes=64)
+            nc.vector.quantize_mx(out=ac_t[c][:].bitcast(FP8X4), scales=as_t[c][:], in_=ag_t[c][:])
+
+        def output(c):
+            ost = work.tile([P, 4096], F32, tag="ost", bufs=3, name="ost")
+            share = VEC_SHARE.get(c, ())
+            for t in range(4):
+                for nh in range(2):
+                    bank = psum.tile([P, 512], F32, tag="bank", name="obank")
+                    for e in range(2):
+                        a0 = 512 * e + 128 * t
+                        p0 = 1024 * e + 512 * nh
+                        nc.tensor.matmul_mx(
+                            out=bank[:],
+                            lhsT=ac_t[c][:, a0 : a0 + 128].bitcast(FP8X4),
+                            lhsT_scale=as_t[c][:, a0 : a0 + 128],
+                            rhs=pc[:, p0 : p0 + 512].bitcast(FP8X4),
+                            rhs_scale=ps[:, p0 : p0 + 512],
+                            start=(e == 0),
+                            stop=(e == 1),
+                        )
+                    dst = ost[:, 1024 * t + 512 * nh : 1024 * t + 512 * (nh + 1)]
+                    if 2 * t + nh in share:
+                        nc.vector.tensor_copy(out=dst, in_=bank[:])
+                    else:
+                        nc.scalar.copy(out=dst, in_=bank[:])
+                if c == NCH - 1:
+                    nc.sync.dma_start(
+                        out=out_v[c][:, 1024 * t : 1024 * (t + 1)], in_=ost[:, 1024 * t : 1024 * (t + 1)]
+                    )
+                elif t % 2 == 1:
+                    nc.sync.dma_start(
+                        out=out_v[c][:, 1024 * (t - 1) : 1024 * (t + 1)],
+                        in_=ost[:, 1024 * (t - 1) : 1024 * (t + 1)],
+                    )
+
+        nc.scalar.activation(out=etemp[:], in_=lt_b[:], func=AF.Exp)
+        nc.vector.tensor_scalar(out=temp[:], in0=etemp[:], scalar1=0.1, scalar2=5.0, op0=ALU.max, op1=ALU.min)
+        nc.vector.reciprocal(out=rtemp[:], in_=temp[:])
+        nc.vector.tensor_reduce(out=twm[:], in_=tw_b[:], axis=AX.X, op=ALU.max)
+        nc.vector.tensor_scalar(out=ntwm[:], in0=twm[:], scalar1=-1.0, scalar2=None, op0=ALU.mult)
+        nc.scalar.activation(out=twx[:], in_=tw_b[:], func=AF.Exp, bias=ntwm[:, 0:1], accum_out=twsum[:, 0:1])
+        nc.scalar.activation(out=twe[:], in_=tw_p[:], func=AF.Exp, bias=ntwm[:, 0:1])
+        nc.vector.tensor_scalar(out=bt[:], in0=sb[:], scalar1=rtemp[:, 0:1], scalar2=None, op0=ALU.mult)
+
+        leaf_max(0)
+        leaf_exp(0)
+        x_load()
+        leaf_max(1)
+        leaf_exp(1)
+        x_load()
+
+        nc.vector.reciprocal(out=rtw[:], in_=twsum[:])
+        nc.vector.tensor_scalar(out=wpos[:], in0=twe[:], scalar1=rtw[:, 0:1], scalar2=None, op0=ALU.mult)
+        nc.vector.tensor_scalar(
+            out=wneg[:], in0=twe[:], scalar1=rtw[:, 0:1], scalar2=-1.0, op0=ALU.mult, op1=ALU.mult
+        )
+
+        wg_t = []
+        for k in range(3):
+            bank = transpose_bank([(w_t[(2 * k + tt) // 3], (2 * k + tt) % 3) for tt in range(2)])
+            wg = work.tile([P, 1024], BF16, tag="wg", bufs=3, name="wg", align_bytes=64)
+            regroup(wg[:].bitcast(F32), bank)
+            wg_t.append(wg)
+        x_load()
+        x_load()
+        x_transpose(0)
+        x_regroup(0)
+
+        leaf_max(2)
+        leaf_exp(2)
+        x_load()
+        leaf_max(3)
+        leaf_exp(3)
+        x_load()
+
+        leaf_rinv(0)
+        leaf_norm(0, 0)
+        for k in range(3):
+            nc.vector.quantize_mx(
+                out=wc[:, 256 * k : 256 * (k + 1)].bitcast(FP8X4),
+                scales=ws[:, 256 * k : 256 * (k + 1)],
+                in_=wg_t[k][:],
+            )
+        leaf_norm(0, 1)
+        x_quant(0)
+        leaf_quant(0)
+
+        x_transpose(1)
+        x_regroup(1)
+
+        leaf_rinv(1)
+        leaf_norm(1, 0)
+        leaf_norm(1, 1)
+        x_quant(1)
+        leaf_quant(1)
+
+        for i in range(NCH + 2):
+            if i < NCH:
+                logits_sigmoid(i)
+                root_planes(i)
+            if i + 2 < NCH:
+                x_transpose(i + 2)
+                x_regroup(i + 2)
+            if i < NCH:
+                path_products(i)
+            if i + 2 < NCH:
+                x_quant(i + 2)
+            if i < NCH:
+                a_quant(i)
+            if i >= 2:
+                output(i - 2)

@@ -153,9 +153,11 @@ def tile_directsofttreeensemble_t_kernel(
 
         def leaf_norm(e, half):
             nc.vector.tensor_tensor(
-                out=pg_t[e][:, 2048 * half : 2048 * (half + 1)].rearrange("p (c j) -> p c j", j=4),
-                in0=ee_t[e][:].rearrange("p (j c) -> p c j", j=4)[:, 512 * half : 512 * (half + 1), :],
-                in1=rinv[:, 4 * e : 4 * e + 4].unsqueeze(1).to_broadcast([P, 512, 4]),
+                out=pg_t[e][:, 2048 * half : 2048 * (half + 1)].rearrange("p (c i j) -> p c j i", i=4, j=4),
+                in0=ee_t[e][:]
+                .rearrange("p (j n) -> p j n", j=4)[:, :, 512 * half : 512 * (half + 1)]
+                .rearrange("p j (c i) -> p c j i", i=4),
+                in1=rinv[:, 4 * e : 4 * e + 4].unsqueeze(1).unsqueeze(3).to_broadcast([P, 128, 4, 4]),
                 op=ALU.mult,
             )
 
@@ -187,8 +189,9 @@ def tile_directsofttreeensemble_t_kernel(
         def logits_sigmoid(c):
             root_t[c] = work.tile([P, 1024], F32, tag="root", bufs=3, name="root")
             child_t[c] = work.tile([P, 2048], F32, tag="child", bufs=3, name="child")
+            child4 = child_t[c][:].rearrange("p (c j i) -> p j c i", j=4, i=4)
             for m in (0, 3, 1, 2, 4, 5):
-                th, i = m // 3, m % 3
+                th, nd = m // 3, m % 3
                 bank = psum.tile([P, 512], F32, tag="bank", name="zbank")
                 nc.tensor.matmul_mx(
                     out=bank[:],
@@ -199,25 +202,26 @@ def tile_directsofttreeensemble_t_kernel(
                     start=True,
                     stop=True,
                 )
-                if i == 0:
-                    dst = root_t[c][:, 512 * th : 512 * (th + 1)]
+                if nd == 0:
+                    dst = root_t[c][:, 512 * th : 512 * (th + 1)].rearrange("p (c i) -> p c i", i=4)
                 else:
-                    j = 2 * th + i - 1
-                    dst = child_t[c][:, 512 * j : 512 * (j + 1)]
+                    dst = child4[:, 2 * th + nd - 1]
                 nc.scalar.activation(
-                    out=dst, in_=bank[:], func=AF.Sigmoid, bias=bt[:, m : m + 1], scale=rtemp[:, 0:1]
+                    out=dst, in_=bank[:].rearrange("p (i c) -> p c i", i=4), func=AF.Sigmoid,
+                    bias=bt[:, m : m + 1], scale=rtemp[:, 0:1],
                 )
 
         def root_planes(c):
             nn_t[c] = work.tile([P, 2048], F32, tag="nn", bufs=2, name="nn")
+            nn4 = nn_t[c][:].rearrange("p (c j i) -> p j c i", j=4, i=4)
             for th in range(2):
-                s0 = root_t[c][:, 512 * th : 512 * (th + 1)]
+                s0 = root_t[c][:, 512 * th : 512 * (th + 1)].rearrange("p (c i) -> p c i", i=4)
                 nc.vector.tensor_scalar(
-                    out=nn_t[c][:, 512 * (2 * th) : 512 * (2 * th + 1)], in0=s0,
+                    out=nn4[:, 2 * th], in0=s0,
                     scalar1=-1.0, scalar2=wpos[:, th : th + 1], op0=ALU.add, op1=ALU.mult,
                 )
                 nc.vector.tensor_scalar(
-                    out=nn_t[c][:, 512 * (2 * th + 1) : 512 * (2 * th + 2)], in0=s0,
+                    out=nn4[:, 2 * th + 1], in0=s0,
                     scalar1=wneg[:, th : th + 1], scalar2=None, op0=ALU.mult,
                 )
 
@@ -225,10 +229,10 @@ def tile_directsofttreeensemble_t_kernel(
             ag_t[c] = work.tile([P, 4096], BF16, tag="ag", bufs=3, name="ag", align_bytes=64)
             for e in range(2):
                 nc.vector.scalar_tensor_tensor(
-                    out=ag_t[c][:, 2048 * e : 2048 * (e + 1)].rearrange("p (b j) -> p b j", j=4),
-                    in0=child_t[c][:].rearrange("p (j b) -> p b j", j=4),
+                    out=ag_t[c][:, 2048 * e : 2048 * (e + 1)].rearrange("p (i m) -> p m i", i=4),
+                    in0=child_t[c][:].rearrange("p (m i) -> p m i", i=4),
                     scalar=-1.0,
-                    in1=nn_t[c][:].rearrange("p (j b) -> p b j", j=4),
+                    in1=nn_t[c][:].rearrange("p (m i) -> p m i", i=4),
                     op0=(ALU.mult if e == 1 else ALU.add),
                     op1=ALU.mult,
                 )

@@ -19,7 +19,7 @@ NCH = B // NB
 FLOPS = 2 * B * D * (3 * T) + 2 * B * (4 * T) * C
 
 MANUAL = True
-VEC_SHARE = {6: (5, 7), 7: (1, 3, 5, 7)}
+VEC_SHARE = {0: (7,), 1: (7,), 2: (7,), 3: (7,), 4: (7,), 5: (7,), 6: (5, 7), 7: (1, 3, 5, 7)}
 
 
 def tile_directsofttreeensemble_t_kernel(

@@ -18,8 +18,8 @@ NB = 512
 NCH = B // NB
 FLOPS = 2 * B * D * (3 * T) + 2 * B * (4 * T) * C
 
-MANUAL = True
-VEC_SHARE = {0: (7,), 1: (7,), 2: (7,), 3: (7,), 4: (7,), 5: (7,), 6: (5, 7), 7: (1, 3, 5, 7)}
+ACCUM_MAX = True
+SPLIT_LAST = True
 
 
 def tile_directsofttreeensemble_t_kernel(
@@ -27,8 +27,7 @@ def tile_directsofttreeensemble_t_kernel(
 ):
     nc = tc.nc
     with ExitStack() as ctx:
-        if MANUAL:
-            ctx.enter_context(tc.manual_schedule())
+        ctx.enter_context(tc.manual_schedule())
         const = ctx.enter_context(tc.tile_pool(name="const", bufs=1))
         work = ctx.enter_context(tc.tile_pool(name="work", bufs=2))
         psum = ctx.enter_context(tc.psum_pool(name="psum", bufs=8))
@@ -52,6 +51,7 @@ def tile_directsofttreeensemble_t_kernel(
         twe = const.tile([P, 2], F32, name="twe")
         wpos = const.tile([P, 2], F32, name="wpos")
         wneg = const.tile([P, 2], F32, name="wneg")
+        mxall = const.tile([P, 8], F32, name="mxall")
         nmax = const.tile([P, 8], F32, name="nmax")
         sums = const.tile([P, 8], F32, name="sums")
         rinv = const.tile([P, 8], F32, name="rinv")
@@ -69,10 +69,13 @@ def tile_directsofttreeensemble_t_kernel(
         leaf_t = []
         for k in range(4):
             lp = work.tile([P, 2048], BF16, tag="raw", bufs=8, name="lp")
-            nc.sync.dma_start(
-                out=lp[:].rearrange("p (r c) -> p r c", r=2),
-                in_=leaf_v[:, 2 * (k % 2) : 2 * (k % 2) + 2, k // 2, :],
-            )
+            lp3 = lp[:].rearrange("p (r c) -> p r c", r=2)
+            j0 = 2 * (k % 2)
+            if k == 0:
+                for r in range(2):
+                    nc.sync.dma_start(out=lp3[:, r : r + 1, :], in_=leaf_v[:, j0 + r : j0 + r + 1, k // 2, :])
+            else:
+                nc.sync.dma_start(out=lp3, in_=leaf_v[:, j0 : j0 + 2, k // 2, :])
             leaf_t.append(lp)
         w_v = split_weights.rearrange("(p t) i d -> p (t i d)", t=2)
         w_t = []
@@ -113,17 +116,24 @@ def tile_directsofttreeensemble_t_kernel(
             )
 
         def leaf_max(k):
-            e, jj = k // 2, k % 2
-            lp3 = leaf_t[k][:].rearrange("p (r c) -> p r c", r=2)
-            m1 = work.tile([P, 2, 512], BF16, tag="m1", name="m1")
-            nc.vector.tensor_tensor(out=m1[:], in0=lp3[:, :, 0:512], in1=lp3[:, :, 512:1024], op=ALU.max)
-            m2 = work.tile([P, 2, 256], BF16, tag="m2", name="m2")
-            nc.vector.tensor_tensor(out=m2[:], in0=m1[:, :, 0:256], in1=m1[:, :, 256:512], op=ALU.max)
-            mx = work.tile([P, 2], F32, tag="mx", name="mx")
-            nc.vector.tensor_reduce(out=mx[:], in_=m2[:], axis=AX.X, op=ALU.max)
-            col = 4 * e + 2 * jj
+            col = 4 * (k // 2) + 2 * (k % 2)
+            if ACCUM_MAX:
+                for r in range(2):
+                    junk = work.tile([P, 1024], BF16, tag="junk", name="junk")
+                    nc.vector.tensor_scalar(
+                        out=junk[:], in0=leaf_t[k][:, 1024 * r : 1024 * (r + 1)], scalar1=1.0, scalar2=None,
+                        op0=ALU.mult, op1=ALU.max, accum_out=mxall[:, col + r : col + r + 1],
+                    )
+            else:
+                nc.vector.tensor_reduce(
+                    out=mxall[:, col : col + 2], in_=leaf_t[k][:].rearrange("p (r c) -> p r c", r=2),
+                    axis=AX.X, op=ALU.max,
+                )
+
+        def leaf_nmax(k):
+            col = 4 * (k // 2) + 2 * (k % 2)
             nc.vector.tensor_scalar(
-                out=nmax[:, col : col + 2], in0=mx[:], scalar1=rtemp[:, 0:1], scalar2=-1.0,
+                out=nmax[:, col : col + 2], in0=mxall[:, col : col + 2], scalar1=rtemp[:, 0:1], scalar2=-1.0,
                 op0=ALU.mult, op1=ALU.mult,
             )
 
@@ -180,8 +190,8 @@ def tile_directsofttreeensemble_t_kernel(
                 regroup(xg32[:, 512 * g : 512 * (g + 1)], xbank[c][g])
 
         def x_quant(c):
-            xc_t[c] = work.tile([P, 512], U32, tag="xc", bufs=3, name="xc", align_bytes=64)
-            xs_t[c] = work.tile([P, 512], U8, tag="xs", bufs=3, name="xs", align_bytes=64)
+            xc_t[c] = work.tile([P, 512], U32, tag="xc", bufs=4, name="xc", align_bytes=64)
+            xs_t[c] = work.tile([P, 512], U8, tag="xs", bufs=4, name="xs", align_bytes=64)
             nc.vector.quantize_mx(out=xc_t[c][:].bitcast(FP8X4), scales=xs_t[c][:], in_=xg_t[c][:])
 
         root_t, child_t, nn_t, ag_t, ac_t, as_t = {}, {}, {}, {}, {}, {}
@@ -225,77 +235,79 @@ def tile_directsofttreeensemble_t_kernel(
                     scalar1=wneg[:, th : th + 1], scalar2=None, op0=ALU.mult,
                 )
 
-        def path_products(c):
+        def a_tiles(c):
             ag_t[c] = work.tile([P, 4096], BF16, tag="ag", bufs=3, name="ag", align_bytes=64)
-            for e in range(2):
-                nc.vector.scalar_tensor_tensor(
-                    out=ag_t[c][:, 2048 * e : 2048 * (e + 1)].rearrange("p (i m) -> p m i", i=4),
-                    in0=child_t[c][:].rearrange("p (m i) -> p m i", i=4),
-                    scalar=-1.0,
-                    in1=nn_t[c][:].rearrange("p (m i) -> p m i", i=4),
-                    op0=(ALU.mult if e == 1 else ALU.add),
-                    op1=ALU.mult,
-                )
-
-        def a_quant(c):
             ac_t[c] = work.tile([P, 1024], U32, tag="ac", bufs=4, name="ac", align_bytes=64)
             as_t[c] = work.tile([P, 1024], U8, tag="as", bufs=4, name="asc", align_bytes=64)
-            nc.vector.quantize_mx(out=ac_t[c][:].bitcast(FP8X4), scales=as_t[c][:], in_=ag_t[c][:])
 
-        def output(c):
-            ost = work.tile([P, 4096], F32, tag="ost", bufs=3, name="ost")
-            share = VEC_SHARE.get(c, ())
-            for t in range(4):
-                for nh in range(2):
-                    bank = psum.tile([P, 512], F32, tag="bank", name="obank")
-                    for e in range(2):
-                        a0 = 512 * e + 128 * t
-                        p0 = 1024 * e + 512 * nh
-                        nc.tensor.matmul_mx(
-                            out=bank[:],
-                            lhsT=ac_t[c][:, a0 : a0 + 128].bitcast(FP8X4),
-                            lhsT_scale=as_t[c][:, a0 : a0 + 128],
-                            rhs=pc[:, p0 : p0 + 512].bitcast(FP8X4),
-                            rhs_scale=ps[:, p0 : p0 + 512],
-                            start=(e == 0),
-                            stop=(e == 1),
-                        )
-                    dst = ost[:, 1024 * t + 512 * nh : 1024 * t + 512 * (nh + 1)]
-                    if 2 * t + nh in share:
-                        nc.vector.tensor_copy(out=dst, in_=bank[:])
-                    else:
-                        nc.scalar.copy(out=dst, in_=bank[:])
-                if c == NCH - 1:
-                    nc.sync.dma_start(
-                        out=out_v[c][:, 1024 * t : 1024 * (t + 1)], in_=ost[:, 1024 * t : 1024 * (t + 1)]
+        def path_product(c, e, part, parts):
+            ni = 4 // parts
+            w = 512 * ni
+            o0 = (2 * part + e) * w
+            nc.vector.scalar_tensor_tensor(
+                out=ag_t[c][:, o0 : o0 + w].rearrange("p (i m) -> p m i", i=ni),
+                in0=child_t[c][:].rearrange("p (m i) -> p m i", i=4)[:, :, ni * part : ni * (part + 1)],
+                scalar=-1.0,
+                in1=nn_t[c][:].rearrange("p (m i) -> p m i", i=4)[:, :, ni * part : ni * (part + 1)],
+                op0=(ALU.mult if e == 1 else ALU.add),
+                op1=ALU.mult,
+            )
+
+        def a_quant(c, part, parts):
+            w = 4096 // parts
+            nc.vector.quantize_mx(
+                out=ac_t[c][:, (w // 4) * part : (w // 4) * (part + 1)].bitcast(FP8X4),
+                scales=as_t[c][:, (w // 4) * part : (w // 4) * (part + 1)],
+                in_=ag_t[c][:, w * part : w * (part + 1)],
+            )
+
+        ost_t = {}
+
+        def output(c, t, parts):
+            if t == 0:
+                ost_t[c] = work.tile([P, 4096], F32, tag="ost", bufs=3, name="ost")
+            ost = ost_t[c]
+            tp = 4 // parts
+            for nh in range(2):
+                bank = psum.tile([P, 512], F32, tag="bank", name="obank")
+                for e in range(2):
+                    a0 = (2 * (t // tp) + e) * 128 * tp + 128 * (t % tp)
+                    p0 = 1024 * e + 512 * nh
+                    nc.tensor.matmul_mx(
+                        out=bank[:],
+                        lhsT=ac_t[c][:, a0 : a0 + 128].bitcast(FP8X4),
+                        lhsT_scale=as_t[c][:, a0 : a0 + 128],
+                        rhs=pc[:, p0 : p0 + 512].bitcast(FP8X4),
+                        rhs_scale=ps[:, p0 : p0 + 512],
+                        start=(e == 0),
+                        stop=(e == 1),
                     )
-                elif t % 2 == 1:
-                    nc.sync.dma_start(
-                        out=out_v[c][:, 1024 * (t - 1) : 1024 * (t + 1)],
-                        in_=ost[:, 1024 * (t - 1) : 1024 * (t + 1)],
-                    )
+                nc.scalar.copy(out=ost[:, 1024 * t + 512 * nh : 1024 * t + 512 * (nh + 1)], in_=bank[:])
+            if c == NCH - 1:
+                nc.sync.dma_start(out=out_v[c][:, 1024 * t : 1024 * (t + 1)], in_=ost[:, 1024 * t : 1024 * (t + 1)])
+            elif t % 2 == 1:
+                nc.sync.dma_start(
+                    out=out_v[c][:, 1024 * (t - 1) : 1024 * (t + 1)], in_=ost[:, 1024 * (t - 1) : 1024 * (t + 1)]
+                )
 
         nc.scalar.activation(out=etemp[:], in_=lt_b[:], func=AF.Exp)
-        nc.vector.tensor_scalar(out=temp[:], in0=etemp[:], scalar1=0.1, scalar2=5.0, op0=ALU.max, op1=ALU.min)
-        nc.vector.reciprocal(out=rtemp[:], in_=temp[:])
-        nc.vector.tensor_reduce(out=twm[:], in_=tw_b[:], axis=AX.X, op=ALU.max)
-        nc.vector.tensor_scalar(out=ntwm[:], in0=twm[:], scalar1=-1.0, scalar2=None, op0=ALU.mult)
-        nc.scalar.activation(out=twx[:], in_=tw_b[:], func=AF.Exp, bias=ntwm[:, 0:1], accum_out=twsum[:, 0:1])
-        nc.scalar.activation(out=twe[:], in_=tw_p[:], func=AF.Exp, bias=ntwm[:, 0:1])
-        nc.vector.tensor_scalar(out=bt[:], in0=sb[:], scalar1=rtemp[:, 0:1], scalar2=None, op0=ALU.mult)
-
         leaf_max(0)
+        nc.vector.tensor_scalar(out=temp[:], in0=etemp[:], scalar1=0.1, scalar2=5.0, op0=ALU.max, op1=ALU.min)
+        nc.vector.tensor_reduce(out=twm[:], in_=tw_b[:], axis=AX.X, op=ALU.max)
+        nc.vector.reciprocal(out=rtemp[:], in_=temp[:])
+        nc.vector.tensor_scalar(out=ntwm[:], in0=twm[:], scalar1=-1.0, scalar2=None, op0=ALU.mult)
+        leaf_nmax(0)
         leaf_exp(0)
         x_load()
         leaf_max(1)
+        nc.vector.tensor_scalar(out=bt[:], in0=sb[:], scalar1=rtemp[:, 0:1], scalar2=None, op0=ALU.mult)
+        leaf_nmax(1)
         leaf_exp(1)
         x_load()
-
-        nc.vector.reciprocal(out=rtw[:], in_=twsum[:])
-        nc.vector.tensor_scalar(out=wpos[:], in0=twe[:], scalar1=rtw[:, 0:1], scalar2=None, op0=ALU.mult)
-        nc.vector.tensor_scalar(
-            out=wneg[:], in0=twe[:], scalar1=rtw[:, 0:1], scalar2=-1.0, op0=ALU.mult, op1=ALU.mult
-        )
+        leaf_max(2)
+        leaf_max(3)
+        leaf_nmax(2)
+        leaf_nmax(3)
 
         wg_t = []
         for k in range(3):
@@ -308,12 +320,12 @@ def tile_directsofttreeensemble_t_kernel(
         x_transpose(0)
         x_regroup(0)
 
-        leaf_max(2)
         leaf_exp(2)
         x_load()
-        leaf_max(3)
         leaf_exp(3)
         x_load()
+        nc.scalar.activation(out=twx[:], in_=tw_b[:], func=AF.Exp, bias=ntwm[:, 0:1], accum_out=twsum[:, 0:1])
+        nc.scalar.activation(out=twe[:], in_=tw_p[:], func=AF.Exp, bias=ntwm[:, 0:1])
 
         leaf_rinv(0)
         leaf_norm(0, 0)
@@ -329,25 +341,51 @@ def tile_directsofttreeensemble_t_kernel(
 
         x_transpose(1)
         x_regroup(1)
+        x_transpose(2)
+        x_regroup(2)
 
         leaf_rinv(1)
+        nc.vector.reciprocal(out=rtw[:], in_=twsum[:])
         leaf_norm(1, 0)
+        nc.vector.tensor_scalar(out=wpos[:], in0=twe[:], scalar1=rtw[:, 0:1], scalar2=None, op0=ALU.mult)
+        nc.vector.tensor_scalar(
+            out=wneg[:], in0=twe[:], scalar1=rtw[:, 0:1], scalar2=-1.0, op0=ALU.mult, op1=ALU.mult
+        )
         leaf_norm(1, 1)
         x_quant(1)
         leaf_quant(1)
+        x_quant(2)
 
+        def parts_of(c):
+            return 2 if (SPLIT_LAST and c == NCH - 1) else 1
+
+        logits_sigmoid(0)
+        root_planes(0)
         for i in range(NCH + 2):
+            if i + 1 < NCH:
+                logits_sigmoid(i + 1)
+            if i + 3 < NCH:
+                x_transpose(i + 3)
+                x_regroup(i + 3)
+            if 2 <= i < NCH + 1:
+                for t in range(4):
+                    output(i - 2, t, parts_of(i - 2))
             if i < NCH:
-                logits_sigmoid(i)
-                root_planes(i)
-            if i + 2 < NCH:
-                x_transpose(i + 2)
-                x_regroup(i + 2)
-            if i < NCH:
-                path_products(i)
-            if i + 2 < NCH:
-                x_quant(i + 2)
-            if i < NCH:
-                a_quant(i)
-            if i >= 2:
-                output(i - 2)
+                a_tiles(i)
+                if parts_of(i) == 1:
+                    path_product(i, 0, 0, 1)
+                    path_product(i, 1, 0, 1)
+                    if i + 1 < NCH:
+                        root_planes(i + 1)
+                    a_quant(i, 0, 1)
+                else:
+                    path_product(i, 0, 0, 2)
+                    path_product(i, 1, 0, 2)
+                    path_product(i, 0, 1, 2)
+                    a_quant(i, 0, 2)
+                    path_product(i, 1, 1, 2)
+                    a_quant(i, 1, 2)
+            if i + 3 < NCH:
+                x_quant(i + 3)
+        for t in range(4):
+            output(NCH - 1, t, parts_of(NCH - 1))

@@ -20,6 +20,7 @@ FLOPS = 2 * B * D * (3 * T) + 2 * B * (4 * T) * C
 
 ACCUM_MAX = True
 SPLIT_LAST = True
+NACT = (1, 1, 0, 0, 0, 0, 1, 1)
 
 
 def tile_directsofttreeensemble_t_kernel(
@@ -161,13 +162,11 @@ def tile_directsofttreeensemble_t_kernel(
             nc.vector.reciprocal(out=rinv[:, 4 * e : 4 * e + 4], in_=sums[:, 4 * e : 4 * e + 4])
             pg_t[e] = work.tile([P, 4096], BF16, tag="ag", bufs=3, name="pg", align_bytes=64)
 
-        def leaf_norm(e, half):
+        def leaf_norm(e):
             nc.vector.tensor_tensor(
-                out=pg_t[e][:, 2048 * half : 2048 * (half + 1)].rearrange("p (c i j) -> p c j i", i=4, j=4),
-                in0=ee_t[e][:]
-                .rearrange("p (j n) -> p j n", j=4)[:, :, 512 * half : 512 * (half + 1)]
-                .rearrange("p j (c i) -> p c j i", i=4),
-                in1=rinv[:, 4 * e : 4 * e + 4].unsqueeze(1).unsqueeze(3).to_broadcast([P, 128, 4, 4]),
+                out=pg_t[e][:].rearrange("p (c i j) -> p c j i", i=4, j=4),
+                in0=ee_t[e][:].rearrange("p (j c i) -> p c j i", j=4, i=4),
+                in1=rinv[:, 4 * e : 4 * e + 4].unsqueeze(1).unsqueeze(3).to_broadcast([P, 256, 4, 4]),
                 op=ALU.mult,
             )
 
@@ -221,10 +220,20 @@ def tile_directsofttreeensemble_t_kernel(
                     bias=bt[:, m : m + 1], scale=rtemp[:, 0:1],
                 )
 
-        def root_planes(c):
-            nn_t[c] = work.tile([P, 2048], F32, tag="nn", bufs=2, name="nn")
+        def root_planes_scalar(c):
+            nn_t[c] = work.tile([P, 2048], F32, tag="nn", bufs=3, name="nn")
             nn4 = nn_t[c][:].rearrange("p (c j i) -> p j c i", j=4, i=4)
-            for th in range(2):
+            for th in range(NACT[c]):
+                s0 = root_t[c][:, 512 * th : 512 * (th + 1)].rearrange("p (c i) -> p c i", i=4)
+                nc.scalar.activation(
+                    out=nn4[:, 2 * th], in_=s0, func=AF.Identity,
+                    bias=wneg[:, th : th + 1], scale=wpos[:, th : th + 1],
+                )
+                nc.scalar.activation(out=nn4[:, 2 * th + 1], in_=s0, func=AF.Copy, scale=wneg[:, th : th + 1])
+
+        def root_planes(c):
+            nn4 = nn_t[c][:].rearrange("p (c j i) -> p j c i", j=4, i=4)
+            for th in range(NACT[c], 2):
                 s0 = root_t[c][:, 512 * th : 512 * (th + 1)].rearrange("p (c i) -> p c i", i=4)
                 nc.vector.tensor_scalar(
                     out=nn4[:, 2 * th], in0=s0,
@@ -282,9 +291,15 @@ def tile_directsofttreeensemble_t_kernel(
                         start=(e == 0),
                         stop=(e == 1),
                     )
-                nc.scalar.copy(out=ost[:, 1024 * t + 512 * nh : 1024 * t + 512 * (nh + 1)], in_=bank[:])
+                o0 = 1024 * t + 512 * nh
+                nc.scalar.copy(out=ost[:, o0 : o0 + 512], in_=bank[:])
+                if c == NCH - 1 and t == 3:
+                    nc.sync.dma_start(out=out_v[c][:, o0 : o0 + 512], in_=ost[:, o0 : o0 + 512])
             if c == NCH - 1:
-                nc.sync.dma_start(out=out_v[c][:, 1024 * t : 1024 * (t + 1)], in_=ost[:, 1024 * t : 1024 * (t + 1)])
+                if t < 3:
+                    nc.sync.dma_start(
+                        out=out_v[c][:, 1024 * t : 1024 * (t + 1)], in_=ost[:, 1024 * t : 1024 * (t + 1)]
+                    )
             elif t % 2 == 1:
                 nc.sync.dma_start(
                     out=out_v[c][:, 1024 * (t - 1) : 1024 * (t + 1)], in_=ost[:, 1024 * (t - 1) : 1024 * (t + 1)]
@@ -300,7 +315,6 @@ def tile_directsofttreeensemble_t_kernel(
         leaf_exp(0)
         x_load()
         leaf_max(1)
-        nc.vector.tensor_scalar(out=bt[:], in0=sb[:], scalar1=rtemp[:, 0:1], scalar2=None, op0=ALU.mult)
         leaf_nmax(1)
         leaf_exp(1)
         x_load()
@@ -328,14 +342,14 @@ def tile_directsofttreeensemble_t_kernel(
         nc.scalar.activation(out=twe[:], in_=tw_p[:], func=AF.Exp, bias=ntwm[:, 0:1])
 
         leaf_rinv(0)
-        leaf_norm(0, 0)
+        nc.vector.tensor_scalar(out=bt[:], in0=sb[:], scalar1=rtemp[:, 0:1], scalar2=None, op0=ALU.mult)
+        leaf_norm(0)
         for k in range(3):
             nc.vector.quantize_mx(
                 out=wc[:, 256 * k : 256 * (k + 1)].bitcast(FP8X4),
                 scales=ws[:, 256 * k : 256 * (k + 1)],
                 in_=wg_t[k][:],
             )
-        leaf_norm(0, 1)
         x_quant(0)
         leaf_quant(0)
 
@@ -346,12 +360,11 @@ def tile_directsofttreeensemble_t_kernel(
 
         leaf_rinv(1)
         nc.vector.reciprocal(out=rtw[:], in_=twsum[:])
-        leaf_norm(1, 0)
+        leaf_norm(1)
         nc.vector.tensor_scalar(out=wpos[:], in0=twe[:], scalar1=rtw[:, 0:1], scalar2=None, op0=ALU.mult)
         nc.vector.tensor_scalar(
             out=wneg[:], in0=twe[:], scalar1=rtw[:, 0:1], scalar2=-1.0, op0=ALU.mult, op1=ALU.mult
         )
-        leaf_norm(1, 1)
         x_quant(1)
         leaf_quant(1)
         x_quant(2)
@@ -360,10 +373,12 @@ def tile_directsofttreeensemble_t_kernel(
             return 2 if (SPLIT_LAST and c == NCH - 1) else 1
 
         logits_sigmoid(0)
+        root_planes_scalar(0)
         root_planes(0)
         for i in range(NCH + 2):
             if i + 1 < NCH:
                 logits_sigmoid(i + 1)
+                root_planes_scalar(i + 1)
             if i + 3 < NCH:
                 x_transpose(i + 3)
                 x_regroup(i + 3)

@@ -20,7 +20,7 @@ FLOPS = 2 * B * D * (3 * T) + 2 * B * (4 * T) * C
 
 ACCUM_MAX = True
 SPLIT_LAST = True
-NACT = (1, 1, 0, 0, 0, 0, 1, 1)
+NACT = (0, 0, 0, 0, 0, 0, 0, 0)
 
 
 def tile_directsofttreeensemble_t_kernel(
@@ -84,13 +84,13 @@ def tile_directsofttreeensemble_t_kernel(
             wr = work.tile([P, 2048], BF16, tag="raw", bufs=8, name="wr")
             nc.sync.dma_start(out=wr[:, 0:1536], in_=w_v[:, 1536 * k : 1536 * (k + 1)])
             w_t.append(wr)
-        x_v = x.rearrange("(c p t) d -> c p (t d)", p=P, t=4)
+        x_v = x.rearrange("(c t p) d -> c p t d", p=P, t=4)
         out_v = out.rearrange("(c p t) n -> c p (t n)", p=P, t=4)
         x_t = []
 
         def x_load():
             xr = work.tile([P, 2048], BF16, tag="raw", bufs=8, name="xr")
-            nc.sync.dma_start(out=xr[:], in_=x_v[len(x_t)])
+            nc.sync.dma_start(out=xr[:].rearrange("p (t d) -> p t d", t=4), in_=x_v[len(x_t)])
             x_t.append(xr)
 
         x_load()
@@ -216,7 +216,7 @@ def tile_directsofttreeensemble_t_kernel(
                 else:
                     dst = child4[:, 2 * th + nd - 1]
                 nc.scalar.activation(
-                    out=dst, in_=bank[:].rearrange("p (i c) -> p c i", i=4), func=AF.Sigmoid,
+                    out=dst, in_=bank[:].rearrange("p (c i) -> p c i", i=4), func=AF.Sigmoid,
                     bias=bt[:, m : m + 1], scale=rtemp[:, 0:1],
                 )
 

@@ -20,7 +20,6 @@ FLOPS = 2 * B * D * (3 * T) + 2 * B * (4 * T) * C
 
 ACCUM_MAX = True
 SPLIT_LAST = True
-NACT = (0, 0, 0, 0, 0, 0, 0, 0)
 
 
 def tile_directsofttreeensemble_t_kernel(
@@ -62,9 +61,6 @@ def tile_directsofttreeensemble_t_kernel(
         ps = const.tile([P, 2048], U8, name="ps", align_bytes=64)
 
         nc.scalar.dma_start(out=lt_b[:], in_=log_temperature.partition_broadcast(P))
-        nc.scalar.dma_start(out=tw_b[:], in_=tree_weights.partition_broadcast(P))
-        nc.scalar.dma_start(out=tw_p[:], in_=tree_weights.rearrange("(p t) -> p t", t=2))
-        nc.scalar.dma_start(out=sb[:], in_=split_biases.rearrange("(p t) i -> p (t i)", t=2))
 
         leaf_v = leaf_logits.rearrange("(p t) (h e) c -> p (t h) e c", t=2, e=2)
         leaf_t = []
@@ -84,17 +80,20 @@ def tile_directsofttreeensemble_t_kernel(
             wr = work.tile([P, 2048], BF16, tag="raw", bufs=8, name="wr")
             nc.sync.dma_start(out=wr[:, 0:1536], in_=w_v[:, 1536 * k : 1536 * (k + 1)])
             w_t.append(wr)
-        x_v = x.rearrange("(c t p) d -> c p t d", p=P, t=4)
+        x_v = x.rearrange("(c p t) d -> c p (t d)", p=P, t=4)
         out_v = out.rearrange("(c p t) n -> c p (t n)", p=P, t=4)
         x_t = []
 
         def x_load():
             xr = work.tile([P, 2048], BF16, tag="raw", bufs=8, name="xr")
-            nc.sync.dma_start(out=xr[:].rearrange("p (t d) -> p t d", t=4), in_=x_v[len(x_t)])
+            nc.sync.dma_start(out=xr[:], in_=x_v[len(x_t)])
             x_t.append(xr)
 
         x_load()
         x_load()
+        nc.sync.dma_start(out=sb[:], in_=split_biases.rearrange("(p t) i -> p (t i)", t=2))
+        nc.sync.dma_start(out=tw_b[:], in_=tree_weights.partition_broadcast(P))
+        nc.sync.dma_start(out=tw_p[:], in_=tree_weights.rearrange("(p t) -> p t", t=2))
 
         def transpose_bank(sources):
             bank = psum.tile([P, 512], F32, tag="bank", name="tbank")
@@ -162,11 +161,13 @@ def tile_directsofttreeensemble_t_kernel(
             nc.vector.reciprocal(out=rinv[:, 4 * e : 4 * e + 4], in_=sums[:, 4 * e : 4 * e + 4])
             pg_t[e] = work.tile([P, 4096], BF16, tag="ag", bufs=3, name="pg", align_bytes=64)
 
-        def leaf_norm(e):
+        def leaf_norm(e, half):
             nc.vector.tensor_tensor(
-                out=pg_t[e][:].rearrange("p (c i j) -> p c j i", i=4, j=4),
-                in0=ee_t[e][:].rearrange("p (j c i) -> p c j i", j=4, i=4),
-                in1=rinv[:, 4 * e : 4 * e + 4].unsqueeze(1).unsqueeze(3).to_broadcast([P, 256, 4, 4]),
+                out=pg_t[e][:, 2048 * half : 2048 * (half + 1)].rearrange("p (c i j) -> p c j i", i=4, j=4),
+                in0=ee_t[e][:]
+                .rearrange("p (j n) -> p j n", j=4)[:, :, 512 * half : 512 * (half + 1)]
+                .rearrange("p j (c i) -> p c j i", i=4),
+                in1=rinv[:, 4 * e : 4 * e + 4].unsqueeze(1).unsqueeze(3).to_broadcast([P, 128, 4, 4]),
                 op=ALU.mult,
             )
 
@@ -216,24 +217,14 @@ def tile_directsofttreeensemble_t_kernel(
                 else:
                     dst = child4[:, 2 * th + nd - 1]
                 nc.scalar.activation(
-                    out=dst, in_=bank[:].rearrange("p (c i) -> p c i", i=4), func=AF.Sigmoid,
+                    out=dst, in_=bank[:].rearrange("p (i c) -> p c i", i=4), func=AF.Sigmoid,
                     bias=bt[:, m : m + 1], scale=rtemp[:, 0:1],
                 )
 
-        def root_planes_scalar(c):
-            nn_t[c] = work.tile([P, 2048], F32, tag="nn", bufs=3, name="nn")
-            nn4 = nn_t[c][:].rearrange("p (c j i) -> p j c i", j=4, i=4)
-            for th in range(NACT[c]):
-                s0 = root_t[c][:, 512 * th : 512 * (th + 1)].rearrange("p (c i) -> p c i", i=4)
-                nc.scalar.activation(
-                    out=nn4[:, 2 * th], in_=s0, func=AF.Identity,
-                    bias=wneg[:, th : th + 1], scale=wpos[:, th : th + 1],
-                )
-                nc.scalar.activation(out=nn4[:, 2 * th + 1], in_=s0, func=AF.Copy, scale=wneg[:, th : th + 1])
-
         def root_planes(c):
+            nn_t[c] = work.tile([P, 2048], F32, tag="nn", bufs=2, name="nn")
             nn4 = nn_t[c][:].rearrange("p (c j i) -> p j c i", j=4, i=4)
-            for th in range(NACT[c], 2):
+            for th in range(2):
                 s0 = root_t[c][:, 512 * th : 512 * (th + 1)].rearrange("p (c i) -> p c i", i=4)
                 nc.vector.tensor_scalar(
                     out=nn4[:, 2 * th], in0=s0,
@@ -291,15 +282,9 @@ def tile_directsofttreeensemble_t_kernel(
                         start=(e == 0),
                         stop=(e == 1),
                     )
-                o0 = 1024 * t + 512 * nh
-                nc.scalar.copy(out=ost[:, o0 : o0 + 512], in_=bank[:])
-                if c == NCH - 1 and t == 3:
-                    nc.sync.dma_start(out=out_v[c][:, o0 : o0 + 512], in_=ost[:, o0 : o0 + 512])
+                nc.scalar.copy(out=ost[:, 1024 * t + 512 * nh : 1024 * t + 512 * (nh + 1)], in_=bank[:])
             if c == NCH - 1:
-                if t < 3:
-                    nc.sync.dma_start(
-                        out=out_v[c][:, 1024 * t : 1024 * (t + 1)], in_=ost[:, 1024 * t : 1024 * (t + 1)]
-                    )
+                nc.sync.dma_start(out=out_v[c][:, 1024 * t : 1024 * (t + 1)], in_=ost[:, 1024 * t : 1024 * (t + 1)])
             elif t % 2 == 1:
                 nc.sync.dma_start(
                     out=out_v[c][:, 1024 * (t - 1) : 1024 * (t + 1)], in_=ost[:, 1024 * (t - 1) : 1024 * (t + 1)]
@@ -308,9 +293,7 @@ def tile_directsofttreeensemble_t_kernel(
         nc.scalar.activation(out=etemp[:], in_=lt_b[:], func=AF.Exp)
         leaf_max(0)
         nc.vector.tensor_scalar(out=temp[:], in0=etemp[:], scalar1=0.1, scalar2=5.0, op0=ALU.max, op1=ALU.min)
-        nc.vector.tensor_reduce(out=twm[:], in_=tw_b[:], axis=AX.X, op=ALU.max)
         nc.vector.reciprocal(out=rtemp[:], in_=temp[:])
-        nc.vector.tensor_scalar(out=ntwm[:], in0=twm[:], scalar1=-1.0, scalar2=None, op0=ALU.mult)
         leaf_nmax(0)
         leaf_exp(0)
         x_load()
@@ -338,18 +321,16 @@ def tile_directsofttreeensemble_t_kernel(
         x_load()
         leaf_exp(3)
         x_load()
-        nc.scalar.activation(out=twx[:], in_=tw_b[:], func=AF.Exp, bias=ntwm[:, 0:1], accum_out=twsum[:, 0:1])
-        nc.scalar.activation(out=twe[:], in_=tw_p[:], func=AF.Exp, bias=ntwm[:, 0:1])
 
         leaf_rinv(0)
-        nc.vector.tensor_scalar(out=bt[:], in0=sb[:], scalar1=rtemp[:, 0:1], scalar2=None, op0=ALU.mult)
-        leaf_norm(0)
+        leaf_norm(0, 0)
         for k in range(3):
             nc.vector.quantize_mx(
                 out=wc[:, 256 * k : 256 * (k + 1)].bitcast(FP8X4),
                 scales=ws[:, 256 * k : 256 * (k + 1)],
                 in_=wg_t[k][:],
             )
+        leaf_norm(0, 1)
         x_quant(0)
         leaf_quant(0)
 
@@ -359,12 +340,18 @@ def tile_directsofttreeensemble_t_kernel(
         x_regroup(2)
 
         leaf_rinv(1)
+        nc.vector.tensor_reduce(out=twm[:], in_=tw_b[:], axis=AX.X, op=ALU.max)
+        nc.vector.tensor_scalar(out=bt[:], in0=sb[:], scalar1=rtemp[:, 0:1], scalar2=None, op0=ALU.mult)
+        nc.vector.tensor_scalar(out=ntwm[:], in0=twm[:], scalar1=-1.0, scalar2=None, op0=ALU.mult)
+        nc.scalar.activation(out=twx[:], in_=tw_b[:], func=AF.Exp, bias=ntwm[:, 0:1], accum_out=twsum[:, 0:1])
+        nc.scalar.activation(out=twe[:], in_=tw_p[:], func=AF.Exp, bias=ntwm[:, 0:1])
+        leaf_norm(1, 0)
         nc.vector.reciprocal(out=rtw[:], in_=twsum[:])
-        leaf_norm(1)
         nc.vector.tensor_scalar(out=wpos[:], in0=twe[:], scalar1=rtw[:, 0:1], scalar2=None, op0=ALU.mult)
         nc.vector.tensor_scalar(
             out=wneg[:], in0=twe[:], scalar1=rtw[:, 0:1], scalar2=-1.0, op0=ALU.mult, op1=ALU.mult
         )
+        leaf_norm(1, 1)
         x_quant(1)
         leaf_quant(1)
         x_quant(2)
@@ -373,12 +360,10 @@ def tile_directsofttreeensemble_t_kernel(
             return 2 if (SPLIT_LAST and c == NCH - 1) else 1
 
         logits_sigmoid(0)
-        root_planes_scalar(0)
         root_planes(0)
         for i in range(NCH + 2):
             if i + 1 < NCH:
                 logits_sigmoid(i + 1)
-                root_planes_scalar(i + 1)
             if i + 3 < NCH:
                 x_transpose(i + 3)
                 x_regroup(i + 3)

@@ -60,7 +60,7 @@ def tile_directsofttreeensemble_t_kernel(
         pc = const.tile([P, 2048], U32, name="pc", align_bytes=64)
         ps = const.tile([P, 2048], U8, name="ps", align_bytes=64)
 
-        nc.scalar.dma_start(out=lt_b[:], in_=log_temperature.partition_broadcast(P))
+        nc.sync.dma_start(out=lt_b[:], in_=log_temperature.partition_broadcast(P))
 
         leaf_v = leaf_logits.rearrange("(p t) (h e) c -> p (t h) e c", t=2, e=2)
         leaf_t = []
@@ -115,10 +115,10 @@ def tile_directsofttreeensemble_t_kernel(
                 in_=bank[:].rearrange("q (t u b) -> q t b u", t=2, u=2),
             )
 
-        def leaf_max(k):
+        def leaf_max(k, rows=(0, 1)):
             col = 4 * (k // 2) + 2 * (k % 2)
             if ACCUM_MAX:
-                for r in range(2):
+                for r in rows:
                     junk = work.tile([P, 1024], BF16, tag="junk", name="junk")
                     nc.vector.tensor_scalar(
                         out=junk[:], in0=leaf_t[k][:, 1024 * r : 1024 * (r + 1)], scalar1=1.0, scalar2=None,
@@ -130,20 +130,21 @@ def tile_directsofttreeensemble_t_kernel(
                     axis=AX.X, op=ALU.max,
                 )
 
-        def leaf_nmax(k):
-            col = 4 * (k // 2) + 2 * (k % 2)
+        def leaf_nmax(k, rows=(0, 1)):
+            col = 4 * (k // 2) + 2 * (k % 2) + rows[0]
+            n = len(rows)
             nc.vector.tensor_scalar(
-                out=nmax[:, col : col + 2], in0=mxall[:, col : col + 2], scalar1=rtemp[:, 0:1], scalar2=-1.0,
+                out=nmax[:, col : col + n], in0=mxall[:, col : col + n], scalar1=rtemp[:, 0:1], scalar2=-1.0,
                 op0=ALU.mult, op1=ALU.mult,
             )
 
         ee_t = {}
 
-        def leaf_exp(k):
+        def leaf_exp(k, rows=(0, 1)):
             e, jj = k // 2, k % 2
-            if jj == 0:
+            if jj == 0 and rows[0] == 0:
                 ee_t[e] = work.tile([P, 4096], F32, tag="ost", bufs=3, name="ee")
-            for r in range(2):
+            for r in rows:
                 j = 2 * jj + r
                 col = 4 * e + j
                 nc.scalar.activation(
@@ -291,11 +292,14 @@ def tile_directsofttreeensemble_t_kernel(
                 )
 
         nc.scalar.activation(out=etemp[:], in_=lt_b[:], func=AF.Exp)
-        leaf_max(0)
+        leaf_max(0, (0,))
         nc.vector.tensor_scalar(out=temp[:], in0=etemp[:], scalar1=0.1, scalar2=5.0, op0=ALU.max, op1=ALU.min)
         nc.vector.reciprocal(out=rtemp[:], in_=temp[:])
-        leaf_nmax(0)
-        leaf_exp(0)
+        leaf_nmax(0, (0,))
+        leaf_exp(0, (0,))
+        leaf_max(0, (1,))
+        leaf_nmax(0, (1,))
+        leaf_exp(0, (1,))
         x_load()
         leaf_max(1)
         leaf_nmax(1)
@@ -374,6 +378,8 @@ def tile_directsofttreeensemble_t_kernel(
                 a_tiles(i)
                 if parts_of(i) == 1:
                     path_product(i, 0, 0, 1)
+                    if i + 3 < NCH:
+                        x_quant(i + 3)
                     path_product(i, 1, 0, 1)
                     if i + 1 < NCH:
                         root_planes(i + 1)
@@ -385,7 +391,5 @@ def tile_directsofttreeensemble_t_kernel(
                     a_quant(i, 0, 2)
                     path_product(i, 1, 1, 2)
                     a_quant(i, 1, 2)
-            if i + 3 < NCH:
-                x_quant(i + 3)
         for t in range(4):
             output(NCH - 1, t, parts_of(NCH - 1))

from contextlib import ExitStack

import concourse.masks as masks
import concourse.mybir as mybir

F32 = mybir.dt.float32
BF16 = mybir.dt.bfloat16
U32 = mybir.dt.uint32
U8 = mybir.dt.uint8
FP8X4 = mybir.dt.float8_e4m3fn_x4
AF = mybir.ActivationFunctionType
ALU = mybir.AluOpType
AX = mybir.AxisListType

P = 128
B, D, C, T = 4096, 512, 1024, 256
NB = 512
NCH = B // NB
FLOPS = 2 * B * D * (3 * T) + 2 * B * (4 * T) * C

ACCUM_MAX = True
SPLIT_LAST = True


def tile_directsofttreeensemble_t_kernel(
    tc, x, split_weights, split_biases, leaf_logits, tree_weights, log_temperature, out
):
    nc = tc.nc
    with ExitStack() as ctx:
        ctx.enter_context(tc.manual_schedule())
        const = ctx.enter_context(tc.tile_pool(name="const", bufs=1))
        work = ctx.enter_context(tc.tile_pool(name="work", bufs=2))
        psum = ctx.enter_context(tc.psum_pool(name="psum", bufs=8))

        ident = const.tile([P, P], F32, name="ident")
        masks.make_identity(nc, ident[:])

        lt_b = const.tile([P, 1], BF16, name="lt_b")
        tw_b = const.tile([P, T], BF16, name="tw_b")
        tw_p = const.tile([P, 2], BF16, name="tw_p")
        sb = const.tile([P, 6], BF16, name="sb")
        etemp = const.tile([P, 1], F32, name="etemp")
        temp = const.tile([P, 1], F32, name="temp")
        rtemp = const.tile([P, 1], F32, name="rtemp")
        bt = const.tile([P, 6], F32, name="bt")
        twm = const.tile([P, 1], F32, name="twm")
        ntwm = const.tile([P, 1], F32, name="ntwm")
        twx = const.tile([P, T], F32, name="twx")
        twsum = const.tile([P, 1], F32, name="twsum")
        rtw = const.tile([P, 1], F32, name="rtw")
        twe = const.tile([P, 2], F32, name="twe")
        wpos = const.tile([P, 2], F32, name="wpos")
        wneg = const.tile([P, 2], F32, name="wneg")
        mxall = const.tile([P, 8], F32, name="mxall")
        nmax = const.tile([P, 8], F32, name="nmax")
        sums = const.tile([P, 8], F32, name="sums")
        rinv = const.tile([P, 8], F32, name="rinv")
        wc = const.tile([P, 768], U32, name="wc", align_bytes=64)
        ws = const.tile([P, 768], U8, name="ws", align_bytes=64)
        pc = const.tile([P, 2048], U32, name="pc", align_bytes=64)
        ps = const.tile([P, 2048], U8, name="ps", align_bytes=64)

        nc.sync.dma_start(out=lt_b[:], in_=log_temperature.partition_broadcast(P))

        leaf_v = leaf_logits.rearrange("(p t) (h e) c -> p (t h) e c", t=2, e=2)
        leaf_t = []
        for k in range(4):
            lp = work.tile([P, 2048], BF16, tag="raw", bufs=8, name="lp")
            lp3 = lp[:].rearrange("p (r c) -> p r c", r=2)
            j0 = 2 * (k % 2)
            if k == 0:
                for r in range(2):
                    nc.sync.dma_start(out=lp3[:, r : r + 1, :], in_=leaf_v[:, j0 + r : j0 + r + 1, k // 2, :])
            else:
                nc.sync.dma_start(out=lp3, in_=leaf_v[:, j0 : j0 + 2, k // 2, :])
            leaf_t.append(lp)
        w_v = split_weights.rearrange("(p t) i d -> p (t i d)", t=2)
        w_t = []
        for k in range(2):
            wr = work.tile([P, 2048], BF16, tag="raw", bufs=8, name="wr")
            nc.sync.dma_start(out=wr[:, 0:1536], in_=w_v[:, 1536 * k : 1536 * (k + 1)])
            w_t.append(wr)
        x_v = x.rearrange("(c p t) d -> c p (t d)", p=P, t=4)
        out_v = out.rearrange("(c p t) n -> c p (t n)", p=P, t=4)
        x_t = []

        def x_load():
            xr = work.tile([P, 2048], BF16, tag="raw", bufs=8, name="xr")
            nc.sync.dma_start(out=xr[:], in_=x_v[len(x_t)])
            x_t.append(xr)

        x_load()
        x_load()
        nc.sync.dma_start(out=sb[:], in_=split_biases.rearrange("(p t) i -> p (t i)", t=2))
        nc.sync.dma_start(out=tw_b[:], in_=tree_weights.partition_broadcast(P))
        nc.sync.dma_start(out=tw_p[:], in_=tree_weights.rearrange("(p t) -> p t", t=2))

        def transpose_bank(sources):
            bank = psum.tile([P, 512], F32, tag="bank", name="tbank")
            for tt in range(2):
                src, blk = sources[tt]
                src32 = src[:].bitcast(F32)
                for u in range(2):
                    s = 2 * tt + u
                    nc.tensor.transpose(
                        out=bank[:, 128 * s : 128 * (s + 1)],
                        in_=src32[:, 256 * blk + 128 * u : 256 * blk + 128 * (u + 1)],
                        identity=ident[:],
                    )
            return bank

        def regroup(dst32, bank):
            nc.scalar.copy(
                out=dst32.rearrange("q (t b u) -> q t b u", t=2, u=2),
                in_=bank[:].rearrange("q (t u b) -> q t b u", t=2, u=2),
            )

        def leaf_max(k, rows=(0, 1)):
            col = 4 * (k // 2) + 2 * (k % 2)
            if ACCUM_MAX:
                for r in rows:
                    junk = work.tile([P, 1024], BF16, tag="junk", name="junk")
                    nc.vector.tensor_scalar(
                        out=junk[:], in0=leaf_t[k][:, 1024 * r : 1024 * (r + 1)], scalar1=1.0, scalar2=None,
                        op0=ALU.mult, op1=ALU.max, accum_out=mxall[:, col + r : col + r + 1],
                    )
            else:
                nc.vector.tensor_reduce(
                    out=mxall[:, col : col + 2], in_=leaf_t[k][:].rearrange("p (r c) -> p r c", r=2),
                    axis=AX.X, op=ALU.max,
                )

        def leaf_nmax(k, rows=(0, 1)):
            col = 4 * (k // 2) + 2 * (k % 2) + rows[0]
            n = len(rows)
            nc.vector.tensor_scalar(
                out=nmax[:, col : col + n], in0=mxall[:, col : col + n], scalar1=rtemp[:, 0:1], scalar2=-1.0,
                op0=ALU.mult, op1=ALU.mult,
            )

        ee_t = {}

        def leaf_exp(k, rows=(0, 1)):
            e, jj = k // 2, k % 2
            if jj == 0 and rows[0] == 0:
                ee_t[e] = work.tile([P, 4096], F32, tag="ost", bufs=3, name="ee")
            for r in rows:
                j = 2 * jj + r
                col = 4 * e + j
                nc.scalar.activation(
                    out=ee_t[e][:, 1024 * j : 1024 * (j + 1)],
                    in_=leaf_t[k][:, 1024 * r : 1024 * (r + 1)],
                    func=AF.Exp,
                    bias=nmax[:, col : col + 1],
                    scale=rtemp[:, 0:1],
                    accum_out=sums[:, col : col + 1],
                )

        pg_t = {}

        def leaf_rinv(e):
            nc.vector.reciprocal(out=rinv[:, 4 * e : 4 * e + 4], in_=sums[:, 4 * e : 4 * e + 4])
            pg_t[e] = work.tile([P, 4096], BF16, tag="ag", bufs=3, name="pg", align_bytes=64)

        def leaf_norm(e, half):
            nc.vector.tensor_tensor(
                out=pg_t[e][:, 2048 * half : 2048 * (half + 1)].rearrange("p (c i j) -> p c j i", i=4, j=4),
                in0=ee_t[e][:]
                .rearrange("p (j n) -> p j n", j=4)[:, :, 512 * half : 512 * (half + 1)]
                .rearrange("p j (c i) -> p c j i", i=4),
                in1=rinv[:, 4 * e : 4 * e + 4].unsqueeze(1).unsqueeze(3).to_broadcast([P, 128, 4, 4]),
                op=ALU.mult,
            )

        def leaf_quant(e):
            nc.vector.quantize_mx(
                out=pc[:, 1024 * e : 1024 * (e + 1)].bitcast(FP8X4),
                scales=ps[:, 1024 * e : 1024 * (e + 1)],
                in_=pg_t[e][:],
            )

        xbank, xg_t, xc_t, xs_t = {}, {}, {}, {}

        def x_transpose(c):
            xbank[c] = [transpose_bank([(x_t[c], 2 * g), (x_t[c], 2 * g + 1)]) for g in range(2)]

        def x_regroup(c):
            xg_t[c] = work.tile([P, 2048], BF16, tag="xg", bufs=2, name="xg", align_bytes=64)
            xg32 = xg_t[c][:].bitcast(F32)
            for g in range(2):
                regroup(xg32[:, 512 * g : 512 * (g + 1)], xbank[c][g])

        def x_quant(c):
            xc_t[c] = work.tile([P, 512], U32, tag="xc", bufs=4, name="xc", align_bytes=64)
            xs_t[c] = work.tile([P, 512], U8, tag="xs", bufs=4, name="xs", align_bytes=64)
            nc.vector.quantize_mx(out=xc_t[c][:].bitcast(FP8X4), scales=xs_t[c][:], in_=xg_t[c][:])

        root_t, child_t, nn_t, ag_t, ac_t, as_t = {}, {}, {}, {}, {}, {}

        def logits_sigmoid(c):
            root_t[c] = work.tile([P, 1024], F32, tag="root", bufs=3, name="root")
            child_t[c] = work.tile([P, 2048], F32, tag="child", bufs=3, name="child")
            child4 = child_t[c][:].rearrange("p (c j i) -> p j c i", j=4, i=4)
            for m in (0, 3, 1, 2, 4, 5):
                th, nd = m // 3, m % 3
                bank = psum.tile([P, 512], F32, tag="bank", name="zbank")
                nc.tensor.matmul_mx(
                    out=bank[:],
                    lhsT=wc[:, 128 * m : 128 * (m + 1)].bitcast(FP8X4),
                    lhsT_scale=ws[:, 128 * m : 128 * (m + 1)],
                    rhs=xc_t[c][:].bitcast(FP8X4),
                    rhs_scale=xs_t[c][:],
                    start=True,
                    stop=True,
                )
                if nd == 0:
                    dst = root_t[c][:, 512 * th : 512 * (th + 1)].rearrange("p (c i) -> p c i", i=4)
                else:
                    dst = child4[:, 2 * th + nd - 1]
                nc.scalar.activation(
                    out=dst, in_=bank[:].rearrange("p (i c) -> p c i", i=4), func=AF.Sigmoid,
                    bias=bt[:, m : m + 1], scale=rtemp[:, 0:1],
                )

        def root_planes(c):
            nn_t[c] = work.tile([P, 2048], F32, tag="nn", bufs=2, name="nn")
            nn4 = nn_t[c][:].rearrange("p (c j i) -> p j c i", j=4, i=4)
            for th in range(2):
                s0 = root_t[c][:, 512 * th : 512 * (th + 1)].rearrange("p (c i) -> p c i", i=4)
                nc.vector.tensor_scalar(
                    out=nn4[:, 2 * th], in0=s0,
                    scalar1=-1.0, scalar2=wpos[:, th : th + 1], op0=ALU.add, op1=ALU.mult,
                )
                nc.vector.tensor_scalar(
                    out=nn4[:, 2 * th + 1], in0=s0,
                    scalar1=wneg[:, th : th + 1], scalar2=None, op0=ALU.mult,
                )

        def a_tiles(c):
            ag_t[c] = work.tile([P, 4096], BF16, tag="ag", bufs=3, name="ag", align_bytes=64)
            ac_t[c] = work.tile([P, 1024], U32, tag="ac", bufs=4, name="ac", align_bytes=64)
            as_t[c] = work.tile([P, 1024], U8, tag="as", bufs=4, name="asc", align_bytes=64)

        def path_product(c, e, part, parts):
            ni = 4 // parts
            w = 512 * ni
            o0 = (2 * part + e) * w
            nc.vector.scalar_tensor_tensor(
                out=ag_t[c][:, o0 : o0 + w].rearrange("p (i m) -> p m i", i=ni),
                in0=child_t[c][:].rearrange("p (m i) -> p m i", i=4)[:, :, ni * part : ni * (part + 1)],
                scalar=-1.0,
                in1=nn_t[c][:].rearrange("p (m i) -> p m i", i=4)[:, :, ni * part : ni * (part + 1)],
                op0=(ALU.mult if e == 1 else ALU.add),
                op1=ALU.mult,
            )

        def a_quant(c, part, parts):
            w = 4096 // parts
            nc.vector.quantize_mx(
                out=ac_t[c][:, (w // 4) * part : (w // 4) * (part + 1)].bitcast(FP8X4),
                scales=as_t[c][:, (w // 4) * part : (w // 4) * (part + 1)],
                in_=ag_t[c][:, w * part : w * (part + 1)],
            )

        ost_t = {}

        def output(c, t, parts):
            if t == 0:
                ost_t[c] = work.tile([P, 4096], F32, tag="ost", bufs=3, name="ost")
            ost = ost_t[c]
            tp = 4 // parts
            for nh in range(2):
                bank = psum.tile([P, 512], F32, tag="bank", name="obank")
                for e in range(2):
                    a0 = (2 * (t // tp) + e) * 128 * tp + 128 * (t % tp)
                    p0 = 1024 * e + 512 * nh
                    nc.tensor.matmul_mx(
                        out=bank[:],
                        lhsT=ac_t[c][:, a0 : a0 + 128].bitcast(FP8X4),
                        lhsT_scale=as_t[c][:, a0 : a0 + 128],
                        rhs=pc[:, p0 : p0 + 512].bitcast(FP8X4),
                        rhs_scale=ps[:, p0 : p0 + 512],
                        start=(e == 0),
                        stop=(e == 1),
                    )
                nc.scalar.copy(out=ost[:, 1024 * t + 512 * nh : 1024 * t + 512 * (nh + 1)], in_=bank[:])
            if c == NCH - 1:
                nc.sync.dma_start(out=out_v[c][:, 1024 * t : 1024 * (t + 1)], in_=ost[:, 1024 * t : 1024 * (t + 1)])
            elif t % 2 == 1:
                nc.sync.dma_start(
                    out=out_v[c][:, 1024 * (t - 1) : 1024 * (t + 1)], in_=ost[:, 1024 * (t - 1) : 1024 * (t + 1)]
                )

        nc.scalar.activation(out=etemp[:], in_=lt_b[:], func=AF.Exp)
        leaf_max(0, (0,))
        nc.vector.tensor_scalar(out=temp[:], in0=etemp[:], scalar1=0.1, scalar2=5.0, op0=ALU.max, op1=ALU.min)
        nc.vector.reciprocal(out=rtemp[:], in_=temp[:])
        leaf_nmax(0, (0,))
        leaf_exp(0, (0,))
        leaf_max(0, (1,))
        leaf_nmax(0, (1,))
        leaf_exp(0, (1,))
        x_load()
        leaf_max(1)
        leaf_nmax(1)
        leaf_exp(1)
        x_load()
        leaf_max(2)
        leaf_max(3)
        leaf_nmax(2)
        leaf_nmax(3)

        wg_t = []
        for k in range(3):
            bank = transpose_bank([(w_t[(2 * k + tt) // 3], (2 * k + tt) % 3) for tt in range(2)])
            wg = work.tile([P, 1024], BF16, tag="wg", bufs=3, name="wg", align_bytes=64)
            regroup(wg[:].bitcast(F32), bank)
            wg_t.append(wg)
        x_load()
        x_load()
        x_transpose(0)
        x_regroup(0)

        leaf_exp(2)
        x_load()
        leaf_exp(3)
        x_load()

        leaf_rinv(0)
        leaf_norm(0, 0)
        for k in range(3):
            nc.vector.quantize_mx(
                out=wc[:, 256 * k : 256 * (k + 1)].bitcast(FP8X4),
                scales=ws[:, 256 * k : 256 * (k + 1)],
                in_=wg_t[k][:],
            )
        leaf_norm(0, 1)
        x_quant(0)
        leaf_quant(0)

        x_transpose(1)
        x_regroup(1)
        x_transpose(2)
        x_regroup(2)

        leaf_rinv(1)
        nc.vector.tensor_reduce(out=twm[:], in_=tw_b[:], axis=AX.X, op=ALU.max)
        nc.vector.tensor_scalar(out=bt[:], in0=sb[:], scalar1=rtemp[:, 0:1], scalar2=None, op0=ALU.mult)
        nc.vector.tensor_scalar(out=ntwm[:], in0=twm[:], scalar1=-1.0, scalar2=None, op0=ALU.mult)
        nc.scalar.activation(out=twx[:], in_=tw_b[:], func=AF.Exp, bias=ntwm[:, 0:1], accum_out=twsum[:, 0:1])
        nc.scalar.activation(out=twe[:], in_=tw_p[:], func=AF.Exp, bias=ntwm[:, 0:1])
        leaf_norm(1, 0)
        nc.vector.reciprocal(out=rtw[:], in_=twsum[:])
        nc.vector.tensor_scalar(out=wpos[:], in0=twe[:], scalar1=rtw[:, 0:1], scalar2=None, op0=ALU.mult)
        nc.vector.tensor_scalar(
            out=wneg[:], in0=twe[:], scalar1=rtw[:, 0:1], scalar2=-1.0, op0=ALU.mult, op1=ALU.mult
        )
        leaf_norm(1, 1)
        x_quant(1)
        leaf_quant(1)
        x_quant(2)

        def parts_of(c):
            return 2 if (SPLIT_LAST and c == NCH - 1) else 1

        logits_sigmoid(0)
        root_planes(0)
        for i in range(NCH + 2):
            if i + 1 < NCH:
                logits_sigmoid(i + 1)
            if i + 3 < NCH:
                x_transpose(i + 3)
                x_regroup(i + 3)
            if 2 <= i < NCH + 1:
                for t in range(4):
                    output(i - 2, t, parts_of(i - 2))
            if i < NCH:
                a_tiles(i)
                if parts_of(i) == 1:
                    path_product(i, 0, 0, 1)
                    if i + 3 < NCH:
                        x_quant(i + 3)
                    path_product(i, 1, 0, 1)
                    if i + 1 < NCH:
                        root_planes(i + 1)
                    a_quant(i, 0, 1)
                else:
                    path_product(i, 0, 0, 2)
                    path_product(i, 1, 0, 2)
                    path_product(i, 0, 1, 2)
                    a_quant(i, 0, 2)
                    path_product(i, 1, 1, 2)
                    a_quant(i, 1, 2)
        for t in range(4):
            output(NCH - 1, t, parts_of(NCH - 1))
